import numpy as np
import ml_dtypes


def mxq(x, axis, fmt="e4m3"):
    dtype, down = {"e4m3": (ml_dtypes.float8_e4m3fn, 7), "e5m2": (ml_dtypes.float8_e5m2, 14)}[fmt]
    v = np.moveaxis(np.asarray(x, np.float32).astype(ml_dtypes.bfloat16).astype(np.float64), axis, -1)
    blocks = v.reshape(v.shape[:-1] + (-1, 32))
    amax = np.abs(blocks).max(-1, keepdims=True)
    byte = np.maximum(np.where(amax > 0, np.frexp(amax)[1] - 1 + 127, 0) - down, 1)
    scale = np.exp2(byte - 127.0)
    codes = (blocks / scale).astype(np.float32).astype(dtype).astype(np.float64)
    return np.moveaxis((codes * scale).reshape(v.shape), -1, axis)


WIDE = False


def mx_kscale(k):
    if not WIDE:
        return np.ones(k)
    levels = np.array([20, -20, 10, -10, 0])
    a = np.random.permutation(np.resize(levels, k // 512 * 4)).reshape(k // 512, 4)
    idx = np.arange(k)
    return np.exp2(a[idx // 512, idx % 128 // 32])


BF16 = ml_dtypes.bfloat16


def bf(x):
    return np.asarray(x, np.float32).astype(BF16)


def f64(x):
    return np.asarray(x).astype(np.float64)


M, K, P, Q = 4096, 1024, 64, 16
N = P * Q
SCALING = 2.0


def _kron(A, B):
    m, n = A.shape
    p, q = B.shape
    return (A[:, None, :, None] * B[None, :, None, :]).reshape(m * p, n * q)


def setup_inputs():
    up = mx_kscale(N)[::Q]
    u = np.repeat(up, Q)
    x = np.random.standard_normal((M, K))
    ow = np.random.standard_normal((N, K)) / np.sqrt(K) / u[:, None]
    a = np.random.standard_normal((P, K)) / np.sqrt(K) / up[:, None]
    b = np.random.standard_normal((Q, 1)) * 0.25
    sc = 1.5 + 0.1 * np.random.standard_normal(1)
    g = np.random.standard_normal((M, N)) * np.exp2(np.random.randint(-12, 1, (M, 1))) * 8.0 * u
    return {"x": bf(x), "original_weight": bf(ow), "lokr_A": bf(a), "lokr_B": bf(b),
            "scalar": bf(sc), "grad_out": bf(g)}


def reference(x, original_weight, lokr_A, lokr_B, scalar, grad_out):
    delta_W = _kron(f64(lokr_A), f64(lokr_B)) * SCALING
    W_eff = f64(original_weight) + f64(scalar)[0] * delta_W
    return mxq(f64(grad_out), 1, "e5m2") @ mxq(W_eff, 0, "e4m3")

@@ -1,0 +1,198 @@
+from contextlib import ExitStack
+
+import concourse.mybir as mybir
+from concourse.masks import make_identity
+
+F32 = mybir.dt.float32
+BF16 = mybir.dt.bfloat16
+U32 = mybir.dt.uint32
+U8 = mybir.dt.uint8
+E4M3_X4 = mybir.dt.float8_e4m3fn_x4
+E5M2_X4 = mybir.dt.float8_e5m2_x4
+ADD = mybir.AluOpType.add
+SUBTRACT = mybir.AluOpType.subtract
+MULT = mybir.AluOpType.mult
+
+P = 128
+PACK = 4
+TOKENS, FEATURES, COLS = 4096, 1024, 1024
+A_ROWS, B_ROWS = 64, 16
+SCALING = 2.0
+PASSES = FEATURES // (P * PACK)
+BANK = 512
+COL_HALVES = COLS // BANK
+K_CHUNK = BANK // PACK
+ROUND_TILES = 4
+ROUNDS = TOKENS // (P * ROUND_TILES)
+STORE_TILES = 2
+AHEAD = 4
+W_UNITS = PASSES * COL_HALVES
+assert AHEAD == W_UNITS
+
+FLOPS = 2 * TOKENS * FEATURES * COLS
+BYTES = 2 * (TOKENS * FEATURES + FEATURES * COLS + A_ROWS * COLS + B_ROWS + 1) + 4 * TOKENS * COLS
+
+
+def tile_lokrlayer_t_kernel(tc, x, original_weight, lokr_A, lokr_B, scalar, grad_out, out):
+    nc = tc.nc
+    with ExitStack() as ctx:
+        consts = ctx.enter_context(tc.tile_pool(name="consts", bufs=1))
+        weights = ctx.enter_context(tc.tile_pool(name="weights", bufs=1))
+        grads = ctx.enter_context(tc.tile_pool(name="grads", bufs=ROUNDS))
+        grouped_pool = ctx.enter_context(tc.tile_pool(name="grouped", bufs=AHEAD))
+        codes_pool = ctx.enter_context(tc.tile_pool(name="codes", bufs=3))
+        results = ctx.enter_context(tc.tile_pool(name="results", bufs=4))
+        psum_t = ctx.enter_context(tc.psum_pool(name="psum_t", bufs=4))
+        psum_o = ctx.enter_context(tc.psum_pool(name="psum_o", bufs=4))
+        ctx.enter_context(tc.manual_schedule())
+
+        grad_view = grad_out.rearrange("(c p j) n -> c p (j n)", p=P, j=ROUND_TILES)
+        out_view = out.rearrange("(c p j) k -> c p (j k)", p=P, j=ROUND_TILES)
+        weight_view = original_weight.rearrange("(g u p e) k -> g p u (e k)", g=PASSES, u=2, p=P, e=2)
+
+        b_all = consts.tile([P, B_ROWS], BF16)
+        nc.sync.dma_start(out=b_all[:], in_=lokr_B.rearrange("b o -> (b o)").partition_broadcast(P))
+        gain_bf = consts.tile([P, 1], BF16)
+        nc.sync.dma_start(out=gain_bf[:], in_=scalar.partition_broadcast(P))
+        a_twice = consts.tile([P, COLS], BF16)
+        nc.sync.dma_start(out=a_twice[0:A_ROWS, :], in_=lokr_A)
+        nc.sync.dma_start(out=a_twice[A_ROWS:P, :], in_=lokr_A)
+
+        base_w = [weights.tile([P, PACK, COLS], BF16, name="base_w%d" % g) for g in range(PASSES)]
+        grad_sb = [grads.tile([P, ROUND_TILES * FEATURES], BF16, name="grad_sb%d" % c, tag="grad_sb") for c in range(ROUNDS)]
+
+        def load_weight(g):
+            nc.sync.dma_start(out=base_w[g][:].rearrange("p (u e) k -> p u (e k)", e=2), in_=weight_view[g])
+
+        def load_grad(c):
+            nc.sync.dma_start(out=grad_sb[c][:], in_=grad_view[c])
+
+        load_weight(0)
+        load_grad(0)
+        load_weight(1)
+        for c in range(1, ROUNDS):
+            load_grad(c)
+
+        ident = consts.tile([P, P], F32)
+        make_identity(nc, ident[:])
+
+        gain = consts.tile([P, 1], F32)
+        nc.vector.tensor_copy(out=gain[:], in_=gain_bf[:])
+        coef = consts.tile([P, B_ROWS], F32)
+        nc.vector.tensor_scalar(out=coef[:], in0=b_all[:], scalar1=gain[:, 0:1], scalar2=SCALING, op0=MULT, op1=MULT)
+        coef_high = consts.tile([P, B_ROWS], BF16)
+        nc.vector.tensor_copy(out=coef_high[:], in_=coef[:])
+        coef_parts = consts.tile([P, B_ROWS], BF16)
+        nc.vector.tensor_copy(out=coef_parts[0:A_ROWS, :], in_=coef_high[0:A_ROWS, :])
+        nc.vector.tensor_tensor(out=coef_parts[A_ROWS:P, :], in0=coef[A_ROWS:P, :], in1=coef_high[A_ROWS:P, :], op=SUBTRACT)
+        row_of_a = consts.tile([P, A_ROWS], BF16)
+        nc.vector.tensor_tensor(out=row_of_a[:], in0=ident[:, 0:A_ROWS], in1=ident[:, A_ROWS:P], op=ADD)
+        spread = consts.tile([P, 2, A_ROWS * 8], BF16)
+        for e in range(2):
+            nc.vector.tensor_tensor(
+                out=spread[:, e, :].rearrange("r (a i) -> r a i", i=8),
+                in0=row_of_a[:].unsqueeze(2).to_broadcast([P, A_ROWS, 8]),
+                in1=coef_parts[:].rearrange("r (i e) -> r e i", e=2)[:, e, :].unsqueeze(1).to_broadcast([P, A_ROWS, 8]),
+                op=MULT,
+            )
+
+        w_codes = weights.tile([P, PASSES * COLS], U32, align_bytes=64)
+        w_scales = weights.tile([P, PASSES * COLS], U8, align_bytes=64)
+        w_grouped = [weights.tile([P, BANK * PACK], BF16, name="w_grouped%d" % i, align_bytes=64) for i in range(W_UNITS)]
+
+        def form_w(unit):
+            g, h = divmod(unit, COL_HALVES)
+            for chunk in range(BANK // K_CHUNK):
+                k0 = h * BANK + chunk * K_CHUNK
+                update = psum_o.tile([P, PACK, K_CHUNK], F32, tag="bank")
+                for t in range(PACK):
+                    u, e = divmod(t, 2)
+                    nc.tensor.matmul(
+                        out=update[:, t, :],
+                        lhsT=spread[:, e, P * (2 * g + u) : P * (2 * g + u + 1)],
+                        rhs=a_twice[:, k0 : k0 + K_CHUNK],
+                        start=True,
+                        stop=True,
+                    )
+                nc.vector.tensor_tensor(
+                    out=w_grouped[unit][:, chunk * BANK : (chunk + 1) * BANK].rearrange("p (k t) -> p k t", t=PACK),
+                    in0=update[:].rearrange("p t k -> p k t"),
+                    in1=base_w[g][:, :, k0 : k0 + K_CHUNK].rearrange("p t k -> p k t"),
+                    op=ADD,
+                )
+
+        def w_cols(g, h):
+            return slice(g * COLS + h * BANK, g * COLS + (h + 1) * BANK)
+
+        def quantise_w(unit):
+            g, h = divmod(unit, COL_HALVES)
+            nc.vector.quantize_mx(
+                out=w_codes[:, w_cols(g, h)].bitcast(E4M3_X4),
+                scales=w_scales[:, w_cols(g, h)],
+                in_=w_grouped[unit][:],
+            )
+
+        grad_grouped = {}
+        grad_codes = {}
+        grad_scales = {}
+
+        def transpose_round(c):
+            grad_grouped[c] = grouped_pool.tile([P, ROUND_TILES * FEATURES], BF16, name="grad_grouped", align_bytes=64)
+            words_in = grad_sb[c][:].bitcast(F32)
+            words_out = grad_grouped[c][:].bitcast(F32)
+            words = FEATURES // 2
+            flipped = []
+            for j in range(ROUND_TILES):
+                bank = psum_t.tile([P, PACK, P], F32, name="flipped")
+                for s in range(PACK):
+                    nc.tensor.transpose(bank[:, s, :], words_in[:, j * words + s * P : j * words + (s + 1) * P], ident[:])
+                flipped.append(bank)
+            for j in range(ROUND_TILES):
+                nc.scalar.copy(
+                    out=words_out[:, j * words : (j + 1) * words].rearrange("p (g r u) -> p g r u", g=PASSES, u=2),
+                    in_=flipped[j][:].rearrange("p (g u) r -> p g r u", u=2),
+                )
+
+        def quantise_grad(c):
+            grad_codes[c] = codes_pool.tile([P, ROUND_TILES * PASSES * P], U32, name="grad_codes", align_bytes=64)
+            grad_scales[c] = codes_pool.tile([P, ROUND_TILES * PASSES * P], U8, name="grad_scales", align_bytes=64)
+            nc.vector.quantize_mx(out=grad_codes[c][:].bitcast(E5M2_X4), scales=grad_scales[c][:], in_=grad_grouped[c][:])
+
+        def multiply_round(c):
+            for j0 in range(0, ROUND_TILES, STORE_TILES):
+                result = results.tile([P, STORE_TILES * COLS], F32, name="result")
+                for j in range(j0, j0 + STORE_TILES):
+                    for h in range(COL_HALVES):
+                        acc = psum_o.tile([P, BANK], F32, tag="bank")
+                        for g in range(PASSES):
+                            tokens = slice((j * PASSES + g) * P, (j * PASSES + g + 1) * P)
+                            nc.tensor.matmul_mx(
+                                out=acc[:],
+                                lhsT=grad_codes[c][:, tokens].bitcast(E5M2_X4),
+                                lhsT_scale=grad_scales[c][:, tokens],
+                                rhs=w_codes[:, w_cols(g, h)].bitcast(E4M3_X4),
+                                rhs_scale=w_scales[:, w_cols(g, h)],
+                                start=(g == 0),
+                                stop=(g == PASSES - 1),
+                            )
+                        dest = result[:, (j - j0) * COLS + h * BANK : (j - j0) * COLS + (h + 1) * BANK]
+                        if h == 0:
+                            nc.scalar.copy(out=dest, in_=acc[:])
+                        else:
+                            nc.vector.tensor_copy(out=dest, in_=acc[:])
+                nc.sync.dma_start(out=out_view[c][:, j0 * COLS : (j0 + STORE_TILES) * COLS], in_=result[:])
+
+        form_w(0)
+        for i in range(1, W_UNITS):
+            form_w(i)
+            quantise_w(i - 1)
+            transpose_round(i - 1)
+        quantise_grad(0)
+        quantise_w(W_UNITS - 1)
+        transpose_round(AHEAD - 1)
+        for c in range(ROUNDS):
+            if c + AHEAD < ROUNDS:
+                transpose_round(c + AHEAD)
+            if c + 1 < ROUNDS:
+                quantise_grad(c + 1)
+            multiply_round(c)

@@ -25,9 +25,9 @@ K_CHUNK = BANK // PACK
 ROUND_TILES = 4
 ROUNDS = TOKENS // (P * ROUND_TILES)
 STORE_TILES = 2
-AHEAD = 4
 W_UNITS = PASSES * COL_HALVES
-assert AHEAD == W_UNITS
+AHEAD = W_UNITS - 1
+PSUM_BANKS = 8
 
 FLOPS = 2 * TOKENS * FEATURES * COLS
 BYTES = 2 * (TOKENS * FEATURES + FEATURES * COLS + A_ROWS * COLS + B_ROWS + 1) + 4 * TOKENS * COLS
@@ -42,8 +42,7 @@ def tile_lokrlayer_t_kernel(tc, x, original_weight, lokr_A, lokr_B, scalar, grad
         grouped_pool = ctx.enter_context(tc.tile_pool(name="grouped", bufs=AHEAD))
         codes_pool = ctx.enter_context(tc.tile_pool(name="codes", bufs=3))
         results = ctx.enter_context(tc.tile_pool(name="results", bufs=4))
-        psum_t = ctx.enter_context(tc.psum_pool(name="psum_t", bufs=4))
-        psum_o = ctx.enter_context(tc.psum_pool(name="psum_o", bufs=4))
+        psum = ctx.enter_context(tc.psum_pool(name="psum", bufs=PSUM_BANKS))
         ctx.enter_context(tc.manual_schedule())
 
         grad_view = grad_out.rearrange("(c p j) n -> c p (j n)", p=P, j=ROUND_TILES)
@@ -75,6 +74,10 @@ def tile_lokrlayer_t_kernel(tc, x, original_weight, lokr_A, lokr_B, scalar, grad
 
         ident = consts.tile([P, P], F32)
         make_identity(nc, ident[:])
+        ident_bf = consts.tile([P, P], BF16)
+        make_identity(nc, ident_bf[:])
+        row_of_a = consts.tile([P, A_ROWS], BF16)
+        nc.vector.tensor_tensor(out=row_of_a[:], in0=ident[:, 0:A_ROWS], in1=ident[:, A_ROWS:P], op=ADD)
 
         gain = consts.tile([P, 1], F32)
         nc.vector.tensor_copy(out=gain[:], in_=gain_bf[:])
@@ -85,8 +88,6 @@ def tile_lokrlayer_t_kernel(tc, x, original_weight, lokr_A, lokr_B, scalar, grad
         coef_parts = consts.tile([P, B_ROWS], BF16)
         nc.vector.tensor_copy(out=coef_parts[0:A_ROWS, :], in_=coef_high[0:A_ROWS, :])
         nc.vector.tensor_tensor(out=coef_parts[A_ROWS:P, :], in0=coef[A_ROWS:P, :], in1=coef_high[A_ROWS:P, :], op=SUBTRACT)
-        row_of_a = consts.tile([P, A_ROWS], BF16)
-        nc.vector.tensor_tensor(out=row_of_a[:], in0=ident[:, 0:A_ROWS], in1=ident[:, A_ROWS:P], op=ADD)
         spread = consts.tile([P, 2, A_ROWS * 8], BF16)
         for e in range(2):
             nc.vector.tensor_tensor(
@@ -104,7 +105,8 @@ def tile_lokrlayer_t_kernel(tc, x, original_weight, lokr_A, lokr_B, scalar, grad
             g, h = divmod(unit, COL_HALVES)
             for chunk in range(BANK // K_CHUNK):
                 k0 = h * BANK + chunk * K_CHUNK
-                update = psum_o.tile([P, PACK, K_CHUNK], F32, tag="bank")
+                sum_on_vector = chunk % 2 == 0
+                update = psum.tile([P, PACK, K_CHUNK], F32, tag="bank")
                 for t in range(PACK):
                     u, e = divmod(t, 2)
                     nc.tensor.matmul(
@@ -112,14 +114,26 @@ def tile_lokrlayer_t_kernel(tc, x, original_weight, lokr_A, lokr_B, scalar, grad
                         lhsT=spread[:, e, P * (2 * g + u) : P * (2 * g + u + 1)],
                         rhs=a_twice[:, k0 : k0 + K_CHUNK],
                         start=True,
-                        stop=True,
+                        stop=sum_on_vector,
                     )
-                nc.vector.tensor_tensor(
-                    out=w_grouped[unit][:, chunk * BANK : (chunk + 1) * BANK].rearrange("p (k t) -> p k t", t=PACK),
-                    in0=update[:].rearrange("p t k -> p k t"),
-                    in1=base_w[g][:, :, k0 : k0 + K_CHUNK].rearrange("p t k -> p k t"),
-                    op=ADD,
-                )
+                    if not sum_on_vector:
+                        nc.tensor.matmul(
+                            out=update[:, t, :],
+                            lhsT=ident_bf[:],
+                            rhs=base_w[g][:, t, k0 : k0 + K_CHUNK],
+                            start=False,
+                            stop=True,
+                        )
+                dest = w_grouped[unit][:, chunk * BANK : (chunk + 1) * BANK].rearrange("p (k t) -> p k t", t=PACK)
+                if sum_on_vector:
+                    nc.vector.tensor_tensor(
+                        out=dest,
+                        in0=update[:].rearrange("p t k -> p k t"),
+                        in1=base_w[g][:, :, k0 : k0 + K_CHUNK].rearrange("p t k -> p k t"),
+                        op=ADD,
+                    )
+                else:
+                    nc.scalar.copy(out=dest, in_=update[:].rearrange("p t k -> p k t"))
 
         def w_cols(g, h):
             return slice(g * COLS + h * BANK, g * COLS + (h + 1) * BANK)
@@ -143,7 +157,7 @@ def tile_lokrlayer_t_kernel(tc, x, original_weight, lokr_A, lokr_B, scalar, grad
             words = FEATURES // 2
             flipped = []
             for j in range(ROUND_TILES):
-                bank = psum_t.tile([P, PACK, P], F32, name="flipped")
+                bank = psum.tile([P, PACK, P], F32, name="flipped", tag="bank")
                 for s in range(PACK):
                     nc.tensor.transpose(bank[:, s, :], words_in[:, j * words + s * P : j * words + (s + 1) * P], ident[:])
                 flipped.append(bank)
@@ -158,12 +172,12 @@ def tile_lokrlayer_t_kernel(tc, x, original_weight, lokr_A, lokr_B, scalar, grad
             grad_scales[c] = codes_pool.tile([P, ROUND_TILES * PASSES * P], U8, name="grad_scales", align_bytes=64)
             nc.vector.quantize_mx(out=grad_codes[c][:].bitcast(E5M2_X4), scales=grad_scales[c][:], in_=grad_grouped[c][:])
 
-        def multiply_round(c):
-            for j0 in range(0, ROUND_TILES, STORE_TILES):
-                result = results.tile([P, STORE_TILES * COLS], F32, name="result")
-                for j in range(j0, j0 + STORE_TILES):
+        def multiply_round(c, store_tiles):
+            for j0 in range(0, ROUND_TILES, store_tiles):
+                result = results.tile([P, store_tiles * COLS], F32, name="result")
+                for j in range(j0, j0 + store_tiles):
                     for h in range(COL_HALVES):
-                        acc = psum_o.tile([P, BANK], F32, tag="bank")
+                        acc = psum.tile([P, BANK], F32, tag="bank")
                         for g in range(PASSES):
                             tokens = slice((j * PASSES + g) * P, (j * PASSES + g + 1) * P)
                             nc.tensor.matmul_mx(
@@ -180,7 +194,7 @@ def tile_lokrlayer_t_kernel(tc, x, original_weight, lokr_A, lokr_B, scalar, grad
                             nc.scalar.copy(out=dest, in_=acc[:])
                         else:
                             nc.vector.tensor_copy(out=dest, in_=acc[:])
-                nc.sync.dma_start(out=out_view[c][:, j0 * COLS : (j0 + STORE_TILES) * COLS], in_=result[:])
+                nc.sync.dma_start(out=out_view[c][:, j0 * COLS : (j0 + store_tiles) * COLS], in_=result[:])
 
         form_w(0)
         for i in range(1, W_UNITS):
@@ -189,10 +203,9 @@ def tile_lokrlayer_t_kernel(tc, x, original_weight, lokr_A, lokr_B, scalar, grad
             transpose_round(i - 1)
         quantise_grad(0)
         quantise_w(W_UNITS - 1)
-        transpose_round(AHEAD - 1)
         for c in range(ROUNDS):
-            if c + AHEAD < ROUNDS:
-                transpose_round(c + AHEAD)
             if c + 1 < ROUNDS:
                 quantise_grad(c + 1)
-            multiply_round(c)
+            multiply_round(c, STORE_TILES if c + 1 < ROUNDS else 1)
+            if c + AHEAD < ROUNDS:
+                transpose_round(c + AHEAD)

@@ -25,6 +25,7 @@ K_CHUNK = BANK // PACK
 ROUND_TILES = 4
 ROUNDS = TOKENS // (P * ROUND_TILES)
 STORE_TILES = 2
+RUN_TILES = 2
 W_UNITS = PASSES * COL_HALVES
 AHEAD = W_UNITS - 1
 PSUM_BANKS = 8
@@ -150,18 +151,19 @@ def tile_lokrlayer_t_kernel(tc, x, original_weight, lokr_A, lokr_B, scalar, grad
         grad_codes = {}
         grad_scales = {}
 
-        def transpose_round(c):
-            grad_grouped[c] = grouped_pool.tile([P, ROUND_TILES * FEATURES], BF16, name="grad_grouped", align_bytes=64)
+        def transpose_round(c, j_first=0, j_count=ROUND_TILES):
+            if j_first == 0:
+                grad_grouped[c] = grouped_pool.tile([P, ROUND_TILES * FEATURES], BF16, name="grad_grouped", align_bytes=64)
             words_in = grad_sb[c][:].bitcast(F32)
             words_out = grad_grouped[c][:].bitcast(F32)
             words = FEATURES // 2
-            flipped = []
-            for j in range(ROUND_TILES):
+            flipped = {}
+            for j in range(j_first, j_first + j_count):
                 bank = psum.tile([P, PACK, P], F32, name="flipped", tag="bank")
                 for s in range(PACK):
                     nc.tensor.transpose(bank[:, s, :], words_in[:, j * words + s * P : j * words + (s + 1) * P], ident[:])
-                flipped.append(bank)
-            for j in range(ROUND_TILES):
+                flipped[j] = bank
+            for j in range(j_first, j_first + j_count):
                 nc.scalar.copy(
                     out=words_out[:, j * words : (j + 1) * words].rearrange("p (g r u) -> p g r u", g=PASSES, u=2),
                     in_=flipped[j][:].rearrange("p (g u) r -> p g r u", u=2),
@@ -172,8 +174,8 @@ def tile_lokrlayer_t_kernel(tc, x, original_weight, lokr_A, lokr_B, scalar, grad
             grad_scales[c] = codes_pool.tile([P, ROUND_TILES * PASSES * P], U8, name="grad_scales", align_bytes=64)
             nc.vector.quantize_mx(out=grad_codes[c][:].bitcast(E5M2_X4), scales=grad_scales[c][:], in_=grad_grouped[c][:])
 
-        def multiply_round(c, store_tiles):
-            for j0 in range(0, ROUND_TILES, store_tiles):
+        def multiply_round(c, store_tiles, j_first=0, j_count=ROUND_TILES):
+            for j0 in range(j_first, j_first + j_count, store_tiles):
                 result = results.tile([P, store_tiles * COLS], F32, name="result")
                 for j in range(j0, j0 + store_tiles):
                     for h in range(COL_HALVES):
@@ -206,6 +208,7 @@ def tile_lokrlayer_t_kernel(tc, x, original_weight, lokr_A, lokr_B, scalar, grad
         for c in range(ROUNDS):
             if c + 1 < ROUNDS:
                 quantise_grad(c + 1)
-            multiply_round(c, STORE_TILES if c + 1 < ROUNDS else 1)
-            if c + AHEAD < ROUNDS:
-                transpose_round(c + AHEAD)
+            for j_first in range(0, ROUND_TILES, RUN_TILES):
+                multiply_round(c, STORE_TILES if c + 1 < ROUNDS else 1, j_first, RUN_TILES)
+                if c + AHEAD < ROUNDS:
+                    transpose_round(c + AHEAD, j_first, RUN_TILES)

@@ -24,10 +24,13 @@ COL_HALVES = COLS // BANK
 K_CHUNK = BANK // PACK
 ROUND_TILES = 4
 ROUNDS = TOKENS // (P * ROUND_TILES)
-STORE_TILES = 2
-RUN_TILES = 2
+PAIR_TILES = 2
+PAIRS = TOKENS // (P * PAIR_TILES)
+ROUND_PAIRS = ROUND_TILES // PAIR_TILES
+PAIR_BANKS = PAIR_TILES * COL_HALVES
 W_UNITS = PASSES * COL_HALVES
-AHEAD = W_UNITS - 1
+AHEAD = ROUND_PAIRS * (W_UNITS - 1)
+REST = 4
 PSUM_BANKS = 8
 
 FLOPS = 2 * TOKENS * FEATURES * COLS
@@ -42,7 +45,7 @@ def tile_lokrlayer_t_kernel(tc, x, original_weight, lokr_A, lokr_B, scalar, grad
         grads = ctx.enter_context(tc.tile_pool(name="grads", bufs=ROUNDS))
         grouped_pool = ctx.enter_context(tc.tile_pool(name="grouped", bufs=AHEAD))
         codes_pool = ctx.enter_context(tc.tile_pool(name="codes", bufs=3))
-        results = ctx.enter_context(tc.tile_pool(name="results", bufs=4))
+        results = ctx.enter_context(tc.tile_pool(name="results", bufs=6))
         psum = ctx.enter_context(tc.psum_pool(name="psum", bufs=PSUM_BANKS))
         ctx.enter_context(tc.manual_schedule())
 
@@ -150,65 +153,75 @@ def tile_lokrlayer_t_kernel(tc, x, original_weight, lokr_A, lokr_B, scalar, grad
         grad_grouped = {}
         grad_codes = {}
         grad_scales = {}
+        words = FEATURES // 2
 
-        def transpose_round(c, j_first=0, j_count=ROUND_TILES):
-            if j_first == 0:
-                grad_grouped[c] = grouped_pool.tile([P, ROUND_TILES * FEATURES], BF16, name="grad_grouped", align_bytes=64)
+        def transpose_pair(i):
+            c, first = divmod(i * PAIR_TILES, ROUND_TILES)
+            grad_grouped[i] = grouped_pool.tile([P, PAIR_TILES * FEATURES], BF16, name="grad_grouped", align_bytes=64)
             words_in = grad_sb[c][:].bitcast(F32)
-            words_out = grad_grouped[c][:].bitcast(F32)
-            words = FEATURES // 2
-            flipped = {}
-            for j in range(j_first, j_first + j_count):
+            words_out = grad_grouped[i][:].bitcast(F32)
+            flipped = []
+            for j in range(PAIR_TILES):
                 bank = psum.tile([P, PACK, P], F32, name="flipped", tag="bank")
                 for s in range(PACK):
-                    nc.tensor.transpose(bank[:, s, :], words_in[:, j * words + s * P : j * words + (s + 1) * P], ident[:])
-                flipped[j] = bank
-            for j in range(j_first, j_first + j_count):
+                    w0 = (first + j) * words + s * P
+                    nc.tensor.transpose(bank[:, s, :], words_in[:, w0 : w0 + P], ident[:])
+                flipped.append(bank)
+            for j in range(PAIR_TILES):
                 nc.scalar.copy(
                     out=words_out[:, j * words : (j + 1) * words].rearrange("p (g r u) -> p g r u", g=PASSES, u=2),
                     in_=flipped[j][:].rearrange("p (g u) r -> p g r u", u=2),
                 )
 
-        def quantise_grad(c):
-            grad_codes[c] = codes_pool.tile([P, ROUND_TILES * PASSES * P], U32, name="grad_codes", align_bytes=64)
-            grad_scales[c] = codes_pool.tile([P, ROUND_TILES * PASSES * P], U8, name="grad_scales", align_bytes=64)
-            nc.vector.quantize_mx(out=grad_codes[c][:].bitcast(E5M2_X4), scales=grad_scales[c][:], in_=grad_grouped[c][:])
+        def quantise_pair(i):
+            grad_codes[i] = codes_pool.tile([P, PAIR_TILES * PASSES * P], U32, name="grad_codes", align_bytes=64)
+            grad_scales[i] = codes_pool.tile([P, PAIR_TILES * PASSES * P], U8, name="grad_scales", align_bytes=64)
+            nc.vector.quantize_mx(out=grad_codes[i][:].bitcast(E5M2_X4), scales=grad_scales[i][:], in_=grad_grouped[i][:])
 
-        def multiply_round(c, store_tiles, j_first=0, j_count=ROUND_TILES):
-            for j0 in range(j_first, j_first + j_count, store_tiles):
-                result = results.tile([P, store_tiles * COLS], F32, name="result")
-                for j in range(j0, j0 + store_tiles):
-                    for h in range(COL_HALVES):
-                        acc = psum.tile([P, BANK], F32, tag="bank")
-                        for g in range(PASSES):
-                            tokens = slice((j * PASSES + g) * P, (j * PASSES + g + 1) * P)
-                            nc.tensor.matmul_mx(
-                                out=acc[:],
-                                lhsT=grad_codes[c][:, tokens].bitcast(E5M2_X4),
-                                lhsT_scale=grad_scales[c][:, tokens],
-                                rhs=w_codes[:, w_cols(g, h)].bitcast(E4M3_X4),
-                                rhs_scale=w_scales[:, w_cols(g, h)],
-                                start=(g == 0),
-                                stop=(g == PASSES - 1),
-                            )
-                        dest = result[:, (j - j0) * COLS + h * BANK : (j - j0) * COLS + (h + 1) * BANK]
-                        if h == 0:
-                            nc.scalar.copy(out=dest, in_=acc[:])
-                        else:
-                            nc.vector.tensor_copy(out=dest, in_=acc[:])
-                nc.sync.dma_start(out=out_view[c][:, j0 * COLS : (j0 + store_tiles) * COLS], in_=result[:])
+        def multiply_pair(i, store_banks):
+            c, first = divmod(i * PAIR_TILES, ROUND_TILES)
+            for b0 in range(0, PAIR_BANKS, store_banks):
+                result = results.tile([P, store_banks * BANK], F32, name="result")
+                for b in range(b0, b0 + store_banks):
+                    j, h = divmod(b, COL_HALVES)
+                    acc = psum.tile([P, BANK], F32, tag="bank")
+                    for g in range(PASSES):
+                        tokens = slice((j * PASSES + g) * P, (j * PASSES + g + 1) * P)
+                        nc.tensor.matmul_mx(
+                            out=acc[:],
+                            lhsT=grad_codes[i][:, tokens].bitcast(E5M2_X4),
+                            lhsT_scale=grad_scales[i][:, tokens],
+                            rhs=w_codes[:, w_cols(g, h)].bitcast(E4M3_X4),
+                            rhs_scale=w_scales[:, w_cols(g, h)],
+                            start=(g == 0),
+                            stop=(g == PASSES - 1),
+                        )
+                    dest = result[:, (b - b0) * BANK : (b - b0 + 1) * BANK]
+                    if h == 0:
+                        nc.scalar.copy(out=dest, in_=acc[:])
+                    else:
+                        nc.vector.tensor_copy(out=dest, in_=acc[:])
+                col0 = (first * COL_HALVES + b0) * BANK
+                nc.sync.dma_start(out=out_view[c][:, col0 : col0 + store_banks * BANK], in_=result[:])
 
         form_w(0)
-        for i in range(1, W_UNITS):
-            form_w(i)
-            quantise_w(i - 1)
-            transpose_round(i - 1)
-        quantise_grad(0)
+        for unit in range(1, W_UNITS):
+            form_w(unit)
+            quantise_w(unit - 1)
+            for i in range(ROUND_PAIRS * (unit - 1), ROUND_PAIRS * unit):
+                transpose_pair(i)
+        quantise_pair(0)
         quantise_w(W_UNITS - 1)
-        for c in range(ROUNDS):
-            if c + 1 < ROUNDS:
-                quantise_grad(c + 1)
-            for j_first in range(0, ROUND_TILES, RUN_TILES):
-                multiply_round(c, STORE_TILES if c + 1 < ROUNDS else 1, j_first, RUN_TILES)
-                if c + AHEAD < ROUNDS:
-                    transpose_round(c + AHEAD, j_first, RUN_TILES)
+        transposed = AHEAD
+        for i in range(PAIRS):
+            if i + 1 < PAIRS:
+                quantise_pair(i + 1)
+            if transposed < PAIRS:
+                multiply_pair(i, PAIR_BANKS)
+            elif i + 1 < PAIRS:
+                multiply_pair(i, COL_HALVES)
+            else:
+                multiply_pair(i, 1)
+            if transposed < PAIRS and i % REST != REST - 1:
+                transpose_pair(transposed)
+                transposed += 1

@@ -29,9 +29,10 @@ PAIRS = TOKENS // (P * PAIR_TILES)
 ROUND_PAIRS = ROUND_TILES // PAIR_TILES
 PAIR_BANKS = PAIR_TILES * COL_HALVES
 W_UNITS = PASSES * COL_HALVES
-AHEAD = ROUND_PAIRS * (W_UNITS - 1)
+AHEAD = 3 * ROUND_PAIRS
 REST = 4
 PSUM_BANKS = 8
+WARM_UP = 4
 
 FLOPS = 2 * TOKENS * FEATURES * COLS
 BYTES = 2 * (TOKENS * FEATURES + FEATURES * COLS + A_ROWS * COLS + B_ROWS + 1) + 4 * TOKENS * COLS
@@ -76,28 +77,39 @@ def tile_lokrlayer_t_kernel(tc, x, original_weight, lokr_A, lokr_B, scalar, grad
         for c in range(1, ROUNDS):
             load_grad(c)
 
+        zeros = consts.tile([P, BANK], BF16)
+        nc.vector.memset(zeros[:], 0.0)
+        idle_bank = psum.tile([P, BANK], F32, name="idle_bank", tag="bank")
+        for n in range(WARM_UP):
+            nc.tensor.matmul(out=idle_bank[:], lhsT=zeros[:, 0:P], rhs=zeros[:], start=True, stop=True)
+
         ident = consts.tile([P, P], F32)
         make_identity(nc, ident[:])
         ident_bf = consts.tile([P, P], BF16)
         make_identity(nc, ident_bf[:])
+        row_sum = consts.tile([P, A_ROWS], F32)
+        nc.vector.tensor_tensor(out=row_sum[:], in0=ident[:, 0:A_ROWS], in1=ident[:, A_ROWS:P], op=ADD)
         row_of_a = consts.tile([P, A_ROWS], BF16)
-        nc.vector.tensor_tensor(out=row_of_a[:], in0=ident[:, 0:A_ROWS], in1=ident[:, A_ROWS:P], op=ADD)
+        nc.vector.tensor_scalar(out=row_of_a[:], in0=row_sum[:], scalar1=SCALING, scalar2=None, op0=MULT)
 
-        gain = consts.tile([P, 1], F32)
-        nc.vector.tensor_copy(out=gain[:], in_=gain_bf[:])
-        coef = consts.tile([P, B_ROWS], F32)
-        nc.vector.tensor_scalar(out=coef[:], in0=b_all[:], scalar1=gain[:, 0:1], scalar2=SCALING, op0=MULT, op1=MULT)
-        coef_high = consts.tile([P, B_ROWS], BF16)
-        nc.vector.tensor_copy(out=coef_high[:], in_=coef[:])
         coef_parts = consts.tile([P, B_ROWS], BF16)
-        nc.vector.tensor_copy(out=coef_parts[0:A_ROWS, :], in_=coef_high[0:A_ROWS, :])
-        nc.vector.tensor_tensor(out=coef_parts[A_ROWS:P, :], in0=coef[A_ROWS:P, :], in1=coef_high[A_ROWS:P, :], op=SUBTRACT)
+        nc.vector.tensor_scalar(out=coef_parts[:], in0=b_all[:], scalar1=gain_bf[:, 0:1], scalar2=None, op0=MULT)
+        nc.vector.scalar_tensor_tensor(
+            out=coef_parts[A_ROWS:P, :],
+            in0=b_all[A_ROWS:P, :],
+            scalar=gain_bf[A_ROWS:P, 0:1],
+            in1=coef_parts[A_ROWS:P, :],
+            op0=MULT,
+            op1=SUBTRACT,
+        )
         spread = consts.tile([P, 2, A_ROWS * 8], BF16)
-        for e in range(2):
+        block_rows = P // 8
+        for block in range(A_ROWS // block_rows):
+            rows = slice(block * block_rows, (block + 1) * block_rows)
             nc.vector.tensor_tensor(
-                out=spread[:, e, :].rearrange("r (a i) -> r a i", i=8),
-                in0=row_of_a[:].unsqueeze(2).to_broadcast([P, A_ROWS, 8]),
-                in1=coef_parts[:].rearrange("r (i e) -> r e i", e=2)[:, e, :].unsqueeze(1).to_broadcast([P, A_ROWS, 8]),
+                out=spread[:, :, P * block : P * (block + 1)].rearrange("r e (a i) -> r e a i", i=8),
+                in0=row_of_a[:, rows].unsqueeze(1).unsqueeze(3).to_broadcast([P, 2, block_rows, 8]),
+                in1=coef_parts[:].rearrange("r (i e) -> r e i", e=2).unsqueeze(2).to_broadcast([P, 2, block_rows, 8]),
                 op=MULT,
             )
 
@@ -105,39 +117,46 @@ def tile_lokrlayer_t_kernel(tc, x, original_weight, lokr_A, lokr_B, scalar, grad
         w_scales = weights.tile([P, PASSES * COLS], U8, align_bytes=64)
         w_grouped = [weights.tile([P, BANK * PACK], BF16, name="w_grouped%d" % i, align_bytes=64) for i in range(W_UNITS)]
 
-        def form_w(unit):
+        updates = {}
+
+        def start_chunk(unit, chunk):
             g, h = divmod(unit, COL_HALVES)
-            for chunk in range(BANK // K_CHUNK):
-                k0 = h * BANK + chunk * K_CHUNK
-                sum_on_vector = chunk % 2 == 0
-                update = psum.tile([P, PACK, K_CHUNK], F32, tag="bank")
-                for t in range(PACK):
-                    u, e = divmod(t, 2)
+            k0 = h * BANK + chunk * K_CHUNK
+            sum_on_vector = chunk % 2 == 0
+            update = psum.tile([P, PACK, K_CHUNK], F32, name="update", tag="bank")
+            for t in range(PACK):
+                u, e = divmod(t, 2)
+                nc.tensor.matmul(
+                    out=update[:, t, :],
+                    lhsT=spread[:, e, P * (2 * g + u) : P * (2 * g + u + 1)],
+                    rhs=a_twice[:, k0 : k0 + K_CHUNK],
+                    start=True,
+                    stop=sum_on_vector,
+                )
+                if not sum_on_vector:
                     nc.tensor.matmul(
                         out=update[:, t, :],
-                        lhsT=spread[:, e, P * (2 * g + u) : P * (2 * g + u + 1)],
-                        rhs=a_twice[:, k0 : k0 + K_CHUNK],
-                        start=True,
-                        stop=sum_on_vector,
+                        lhsT=ident_bf[:],
+                        rhs=base_w[g][:, t, k0 : k0 + K_CHUNK],
+                        start=False,
+                        stop=True,
                     )
-                    if not sum_on_vector:
-                        nc.tensor.matmul(
-                            out=update[:, t, :],
-                            lhsT=ident_bf[:],
-                            rhs=base_w[g][:, t, k0 : k0 + K_CHUNK],
-                            start=False,
-                            stop=True,
-                        )
-                dest = w_grouped[unit][:, chunk * BANK : (chunk + 1) * BANK].rearrange("p (k t) -> p k t", t=PACK)
-                if sum_on_vector:
-                    nc.vector.tensor_tensor(
-                        out=dest,
-                        in0=update[:].rearrange("p t k -> p k t"),
-                        in1=base_w[g][:, :, k0 : k0 + K_CHUNK].rearrange("p t k -> p k t"),
-                        op=ADD,
-                    )
-                else:
-                    nc.scalar.copy(out=dest, in_=update[:].rearrange("p t k -> p k t"))
+            updates[unit, chunk] = update
+
+        def finish_chunk(unit, chunk):
+            g, h = divmod(unit, COL_HALVES)
+            k0 = h * BANK + chunk * K_CHUNK
+            update = updates[unit, chunk]
+            dest = w_grouped[unit][:, chunk * BANK : (chunk + 1) * BANK].rearrange("p (k t) -> p k t", t=PACK)
+            if chunk % 2 == 0:
+                nc.vector.tensor_tensor(
+                    out=dest,
+                    in0=update[:].rearrange("p t k -> p k t"),
+                    in1=base_w[g][:, :, k0 : k0 + K_CHUNK].rearrange("p t k -> p k t"),
+                    op=ADD,
+                )
+            else:
+                nc.scalar.copy(out=dest, in_=update[:].rearrange("p t k -> p k t"))
 
         def w_cols(g, h):
             return slice(g * COLS + h * BANK, g * COLS + (h + 1) * BANK)
@@ -204,14 +223,32 @@ def tile_lokrlayer_t_kernel(tc, x, original_weight, lokr_A, lokr_B, scalar, grad
                 col0 = (first * COL_HALVES + b0) * BANK
                 nc.sync.dma_start(out=out_view[c][:, col0 : col0 + store_banks * BANK], in_=result[:])
 
-        form_w(0)
-        for unit in range(1, W_UNITS):
-            form_w(unit)
-            quantise_w(unit - 1)
-            for i in range(ROUND_PAIRS * (unit - 1), ROUND_PAIRS * unit):
+        chunks = range(BANK // K_CHUNK)
+
+        def form_pass(g):
+            units = range(g * COL_HALVES, (g + 1) * COL_HALVES)
+            for parity in range(2):
+                for unit in units:
+                    for chunk in chunks[parity::2]:
+                        start_chunk(unit, chunk)
+            for unit in units:
+                for chunk in chunks:
+                    finish_chunk(unit, chunk)
+
+        def transpose_round(c):
+            for i in range(ROUND_PAIRS * c, ROUND_PAIRS * (c + 1)):
                 transpose_pair(i)
+
+        form_pass(0)
+        transpose_round(0)
+        quantise_w(0)
+        quantise_w(1)
         quantise_pair(0)
-        quantise_w(W_UNITS - 1)
+        form_pass(1)
+        transpose_round(1)
+        quantise_w(2)
+        transpose_round(2)
+        quantise_w(3)
         transposed = AHEAD
         for i in range(PAIRS):
             if i + 1 < PAIRS:

@@ -29,10 +29,9 @@ PAIRS = TOKENS // (P * PAIR_TILES)
 ROUND_PAIRS = ROUND_TILES // PAIR_TILES
 PAIR_BANKS = PAIR_TILES * COL_HALVES
 W_UNITS = PASSES * COL_HALVES
-AHEAD = 3 * ROUND_PAIRS
-REST = 4
+AHEAD = 2 * ROUND_PAIRS
+REST = 7
 PSUM_BANKS = 8
-WARM_UP = 4
 
 FLOPS = 2 * TOKENS * FEATURES * COLS
 BYTES = 2 * (TOKENS * FEATURES + FEATURES * COLS + A_ROWS * COLS + B_ROWS + 1) + 4 * TOKENS * COLS
@@ -76,12 +75,6 @@ def tile_lokrlayer_t_kernel(tc, x, original_weight, lokr_A, lokr_B, scalar, grad
         load_weight(1)
         for c in range(1, ROUNDS):
             load_grad(c)
-
-        zeros = consts.tile([P, BANK], BF16)
-        nc.vector.memset(zeros[:], 0.0)
-        idle_bank = psum.tile([P, BANK], F32, name="idle_bank", tag="bank")
-        for n in range(WARM_UP):
-            nc.tensor.matmul(out=idle_bank[:], lhsT=zeros[:, 0:P], rhs=zeros[:], start=True, stop=True)
 
         ident = consts.tile([P, P], F32)
         make_identity(nc, ident[:])
@@ -247,7 +240,6 @@ def tile_lokrlayer_t_kernel(tc, x, original_weight, lokr_A, lokr_B, scalar, grad
         form_pass(1)
         transpose_round(1)
         quantise_w(2)
-        transpose_round(2)
         quantise_w(3)
         transposed = AHEAD
         for i in range(PAIRS):

@@ -45,7 +45,8 @@ def tile_lokrlayer_t_kernel(tc, x, original_weight, lokr_A, lokr_B, scalar, grad
         grads = ctx.enter_context(tc.tile_pool(name="grads", bufs=ROUNDS))
         grouped_pool = ctx.enter_context(tc.tile_pool(name="grouped", bufs=AHEAD))
         codes_pool = ctx.enter_context(tc.tile_pool(name="codes", bufs=3))
-        results = ctx.enter_context(tc.tile_pool(name="results", bufs=6))
+        results = ctx.enter_context(tc.tile_pool(name="results", bufs=4))
+        last_results = ctx.enter_context(tc.tile_pool(name="last_results", bufs=6))
         psum = ctx.enter_context(tc.psum_pool(name="psum", bufs=PSUM_BANKS))
         ctx.enter_context(tc.manual_schedule())
 
@@ -190,31 +191,37 @@ def tile_lokrlayer_t_kernel(tc, x, original_weight, lokr_A, lokr_B, scalar, grad
             grad_scales[i] = codes_pool.tile([P, PAIR_TILES * PASSES * P], U8, name="grad_scales", align_bytes=64)
             nc.vector.quantize_mx(out=grad_codes[i][:].bitcast(E5M2_X4), scales=grad_scales[i][:], in_=grad_grouped[i][:])
 
+        filling = {}
+
         def multiply_pair(i, store_banks):
             c, first = divmod(i * PAIR_TILES, ROUND_TILES)
-            for b0 in range(0, PAIR_BANKS, store_banks):
-                result = results.tile([P, store_banks * BANK], F32, name="result")
-                for b in range(b0, b0 + store_banks):
-                    j, h = divmod(b, COL_HALVES)
-                    acc = psum.tile([P, BANK], F32, tag="bank")
-                    for g in range(PASSES):
-                        tokens = slice((j * PASSES + g) * P, (j * PASSES + g + 1) * P)
-                        nc.tensor.matmul_mx(
-                            out=acc[:],
-                            lhsT=grad_codes[i][:, tokens].bitcast(E5M2_X4),
-                            lhsT_scale=grad_scales[i][:, tokens],
-                            rhs=w_codes[:, w_cols(g, h)].bitcast(E4M3_X4),
-                            rhs_scale=w_scales[:, w_cols(g, h)],
-                            start=(g == 0),
-                            stop=(g == PASSES - 1),
-                        )
-                    dest = result[:, (b - b0) * BANK : (b - b0 + 1) * BANK]
-                    if h == 0:
-                        nc.scalar.copy(out=dest, in_=acc[:])
-                    else:
-                        nc.vector.tensor_copy(out=dest, in_=acc[:])
-                col0 = (first * COL_HALVES + b0) * BANK
-                nc.sync.dma_start(out=out_view[c][:, col0 : col0 + store_banks * BANK], in_=result[:])
+            for b in range(PAIR_BANKS):
+                j, h = divmod(b, COL_HALVES)
+                place = (first * COL_HALVES + b) % store_banks
+                if place == 0:
+                    pool = results if store_banks >= PAIR_BANKS else last_results
+                    filling[0] = pool.tile([P, store_banks * BANK], F32, name="result")
+                result = filling[0]
+                acc = psum.tile([P, BANK], F32, tag="bank")
+                for g in range(PASSES):
+                    tokens = slice((j * PASSES + g) * P, (j * PASSES + g + 1) * P)
+                    nc.tensor.matmul_mx(
+                        out=acc[:],
+                        lhsT=grad_codes[i][:, tokens].bitcast(E5M2_X4),
+                        lhsT_scale=grad_scales[i][:, tokens],
+                        rhs=w_codes[:, w_cols(g, h)].bitcast(E4M3_X4),
+                        rhs_scale=w_scales[:, w_cols(g, h)],
+                        start=(g == 0),
+                        stop=(g == PASSES - 1),
+                    )
+                dest = result[:, place * BANK : (place + 1) * BANK]
+                if h == 0:
+                    nc.scalar.copy(out=dest, in_=acc[:])
+                else:
+                    nc.vector.tensor_copy(out=dest, in_=acc[:])
+                if place == store_banks - 1:
+                    col1 = (first * COL_HALVES + b + 1) * BANK
+                    nc.sync.dma_start(out=out_view[c][:, col1 - store_banks * BANK : col1], in_=result[:])
 
         chunks = range(BANK // K_CHUNK)
 
@@ -245,7 +252,9 @@ def tile_lokrlayer_t_kernel(tc, x, original_weight, lokr_A, lokr_B, scalar, grad
         for i in range(PAIRS):
             if i + 1 < PAIRS:
                 quantise_pair(i + 1)
-            if transposed < PAIRS:
+            if i < PAIRS // 2:
+                multiply_pair(i, ROUND_PAIRS * PAIR_BANKS)
+            elif transposed < PAIRS:
                 multiply_pair(i, PAIR_BANKS)
             elif i + 1 < PAIRS:
                 multiply_pair(i, COL_HALVES)

from contextlib import ExitStack

import concourse.mybir as mybir
from concourse.masks import make_identity

F32 = mybir.dt.float32
BF16 = mybir.dt.bfloat16
U32 = mybir.dt.uint32
U8 = mybir.dt.uint8
E4M3_X4 = mybir.dt.float8_e4m3fn_x4
E5M2_X4 = mybir.dt.float8_e5m2_x4
ADD = mybir.AluOpType.add
SUBTRACT = mybir.AluOpType.subtract
MULT = mybir.AluOpType.mult

P = 128
PACK = 4
TOKENS, FEATURES, COLS = 4096, 1024, 1024
A_ROWS, B_ROWS = 64, 16
SCALING = 2.0
PASSES = FEATURES // (P * PACK)
BANK = 512
COL_HALVES = COLS // BANK
K_CHUNK = BANK // PACK
ROUND_TILES = 4
ROUNDS = TOKENS // (P * ROUND_TILES)
PAIR_TILES = 2
PAIRS = TOKENS // (P * PAIR_TILES)
ROUND_PAIRS = ROUND_TILES // PAIR_TILES
PAIR_BANKS = PAIR_TILES * COL_HALVES
W_UNITS = PASSES * COL_HALVES
AHEAD = 2 * ROUND_PAIRS
REST = 7
PSUM_BANKS = 8

FLOPS = 2 * TOKENS * FEATURES * COLS
BYTES = 2 * (TOKENS * FEATURES + FEATURES * COLS + A_ROWS * COLS + B_ROWS + 1) + 4 * TOKENS * COLS


def tile_lokrlayer_t_kernel(tc, x, original_weight, lokr_A, lokr_B, scalar, grad_out, out):
    nc = tc.nc
    with ExitStack() as ctx:
        consts = ctx.enter_context(tc.tile_pool(name="consts", bufs=1))
        weights = ctx.enter_context(tc.tile_pool(name="weights", bufs=1))
        grads = ctx.enter_context(tc.tile_pool(name="grads", bufs=ROUNDS))
        grouped_pool = ctx.enter_context(tc.tile_pool(name="grouped", bufs=AHEAD))
        codes_pool = ctx.enter_context(tc.tile_pool(name="codes", bufs=3))
        results = ctx.enter_context(tc.tile_pool(name="results", bufs=4))
        last_results = ctx.enter_context(tc.tile_pool(name="last_results", bufs=6))
        psum = ctx.enter_context(tc.psum_pool(name="psum", bufs=PSUM_BANKS))
        ctx.enter_context(tc.manual_schedule())

        grad_view = grad_out.rearrange("(c p j) n -> c p (j n)", p=P, j=ROUND_TILES)
        out_view = out.rearrange("(c p j) k -> c p (j k)", p=P, j=ROUND_TILES)
        weight_view = original_weight.rearrange("(g u p e) k -> g p u (e k)", g=PASSES, u=2, p=P, e=2)

        b_all = consts.tile([P, B_ROWS], BF16)
        nc.sync.dma_start(out=b_all[:], in_=lokr_B.rearrange("b o -> (b o)").partition_broadcast(P))
        gain_bf = consts.tile([P, 1], BF16)
        nc.sync.dma_start(out=gain_bf[:], in_=scalar.partition_broadcast(P))
        a_twice = consts.tile([P, COLS], BF16)
        nc.sync.dma_start(out=a_twice[0:A_ROWS, :], in_=lokr_A)
        nc.sync.dma_start(out=a_twice[A_ROWS:P, :], in_=lokr_A)

        base_w = [weights.tile([P, PACK, COLS], BF16, name="base_w%d" % g) for g in range(PASSES)]
        grad_sb = [grads.tile([P, ROUND_TILES * FEATURES], BF16, name="grad_sb%d" % c, tag="grad_sb") for c in range(ROUNDS)]

        def load_weight(g):
            nc.sync.dma_start(out=base_w[g][:].rearrange("p (u e) k -> p u (e k)", e=2), in_=weight_view[g])

        def load_grad(c):
            nc.sync.dma_start(out=grad_sb[c][:], in_=grad_view[c])

        load_weight(0)
        load_grad(0)
        load_weight(1)
        for c in range(1, ROUNDS):
            load_grad(c)

        ident = consts.tile([P, P], F32)
        make_identity(nc, ident[:])
        ident_bf = consts.tile([P, P], BF16)
        make_identity(nc, ident_bf[:])
        row_sum = consts.tile([P, A_ROWS], F32)
        nc.vector.tensor_tensor(out=row_sum[:], in0=ident[:, 0:A_ROWS], in1=ident[:, A_ROWS:P], op=ADD)
        row_of_a = consts.tile([P, A_ROWS], BF16)
        nc.vector.tensor_scalar(out=row_of_a[:], in0=row_sum[:], scalar1=SCALING, scalar2=None, op0=MULT)

        coef_parts = consts.tile([P, B_ROWS], BF16)
        nc.vector.tensor_scalar(out=coef_parts[:], in0=b_all[:], scalar1=gain_bf[:, 0:1], scalar2=None, op0=MULT)
        nc.vector.scalar_tensor_tensor(
            out=coef_parts[A_ROWS:P, :],
            in0=b_all[A_ROWS:P, :],
            scalar=gain_bf[A_ROWS:P, 0:1],
            in1=coef_parts[A_ROWS:P, :],
            op0=MULT,
            op1=SUBTRACT,
        )
        spread = consts.tile([P, 2, A_ROWS * 8], BF16)
        block_rows = P // 8
        for block in range(A_ROWS // block_rows):
            rows = slice(block * block_rows, (block + 1) * block_rows)
            nc.vector.tensor_tensor(
                out=spread[:, :, P * block : P * (block + 1)].rearrange("r e (a i) -> r e a i", i=8),
                in0=row_of_a[:, rows].unsqueeze(1).unsqueeze(3).to_broadcast([P, 2, block_rows, 8]),
                in1=coef_parts[:].rearrange("r (i e) -> r e i", e=2).unsqueeze(2).to_broadcast([P, 2, block_rows, 8]),
                op=MULT,
            )

        w_codes = weights.tile([P, PASSES * COLS], U32, align_bytes=64)
        w_scales = weights.tile([P, PASSES * COLS], U8, align_bytes=64)
        w_grouped = [weights.tile([P, BANK * PACK], BF16, name="w_grouped%d" % i, align_bytes=64) for i in range(W_UNITS)]

        updates = {}

        def start_chunk(unit, chunk):
            g, h = divmod(unit, COL_HALVES)
            k0 = h * BANK + chunk * K_CHUNK
            sum_on_vector = chunk % 2 == 0
            update = psum.tile([P, PACK, K_CHUNK], F32, name="update", tag="bank")
            for t in range(PACK):
                u, e = divmod(t, 2)
                nc.tensor.matmul(
                    out=update[:, t, :],
                    lhsT=spread[:, e, P * (2 * g + u) : P * (2 * g + u + 1)],
                    rhs=a_twice[:, k0 : k0 + K_CHUNK],
                    start=True,
                    stop=sum_on_vector,
                )
                if not sum_on_vector:
                    nc.tensor.matmul(
                        out=update[:, t, :],
                        lhsT=ident_bf[:],
                        rhs=base_w[g][:, t, k0 : k0 + K_CHUNK],
                        start=False,
                        stop=True,
                    )
            updates[unit, chunk] = update

        def finish_chunk(unit, chunk):
            g, h = divmod(unit, COL_HALVES)
            k0 = h * BANK + chunk * K_CHUNK
            update = updates[unit, chunk]
            dest = w_grouped[unit][:, chunk * BANK : (chunk + 1) * BANK].rearrange("p (k t) -> p k t", t=PACK)
            if chunk % 2 == 0:
                nc.vector.tensor_tensor(
                    out=dest,
                    in0=update[:].rearrange("p t k -> p k t"),
                    in1=base_w[g][:, :, k0 : k0 + K_CHUNK].rearrange("p t k -> p k t"),
                    op=ADD,
                )
            else:
                nc.scalar.copy(out=dest, in_=update[:].rearrange("p t k -> p k t"))

        def w_cols(g, h):
            return slice(g * COLS + h * BANK, g * COLS + (h + 1) * BANK)

        def quantise_w(unit):
            g, h = divmod(unit, COL_HALVES)
            nc.vector.quantize_mx(
                out=w_codes[:, w_cols(g, h)].bitcast(E4M3_X4),
                scales=w_scales[:, w_cols(g, h)],
                in_=w_grouped[unit][:],
            )

        grad_grouped = {}
        grad_codes = {}
        grad_scales = {}
        words = FEATURES // 2

        def transpose_pair(i):
            c, first = divmod(i * PAIR_TILES, ROUND_TILES)
            grad_grouped[i] = grouped_pool.tile([P, PAIR_TILES * FEATURES], BF16, name="grad_grouped", align_bytes=64)
            words_in = grad_sb[c][:].bitcast(F32)
            words_out = grad_grouped[i][:].bitcast(F32)
            flipped = []
            for j in range(PAIR_TILES):
                bank = psum.tile([P, PACK, P], F32, name="flipped", tag="bank")
                for s in range(PACK):
                    w0 = (first + j) * words + s * P
                    nc.tensor.transpose(bank[:, s, :], words_in[:, w0 : w0 + P], ident[:])
                flipped.append(bank)
            for j in range(PAIR_TILES):
                nc.scalar.copy(
                    out=words_out[:, j * words : (j + 1) * words].rearrange("p (g r u) -> p g r u", g=PASSES, u=2),
                    in_=flipped[j][:].rearrange("p (g u) r -> p g r u", u=2),
                )

        def quantise_pair(i):
            grad_codes[i] = codes_pool.tile([P, PAIR_TILES * PASSES * P], U32, name="grad_codes", align_bytes=64)
            grad_scales[i] = codes_pool.tile([P, PAIR_TILES * PASSES * P], U8, name="grad_scales", align_bytes=64)
            nc.vector.quantize_mx(out=grad_codes[i][:].bitcast(E5M2_X4), scales=grad_scales[i][:], in_=grad_grouped[i][:])

        filling = {}

        def multiply_pair(i, store_banks):
            c, first = divmod(i * PAIR_TILES, ROUND_TILES)
            for b in range(PAIR_BANKS):
                j, h = divmod(b, COL_HALVES)
                place = (first * COL_HALVES + b) % store_banks
                if place == 0:
                    pool = results if store_banks >= PAIR_BANKS else last_results
                    filling[0] = pool.tile([P, store_banks * BANK], F32, name="result")
                result = filling[0]
                acc = psum.tile([P, BANK], F32, tag="bank")
                for g in range(PASSES):
                    tokens = slice((j * PASSES + g) * P, (j * PASSES + g + 1) * P)
                    nc.tensor.matmul_mx(
                        out=acc[:],
                        lhsT=grad_codes[i][:, tokens].bitcast(E5M2_X4),
                        lhsT_scale=grad_scales[i][:, tokens],
                        rhs=w_codes[:, w_cols(g, h)].bitcast(E4M3_X4),
                        rhs_scale=w_scales[:, w_cols(g, h)],
                        start=(g == 0),
                        stop=(g == PASSES - 1),
                    )
                dest = result[:, place * BANK : (place + 1) * BANK]
                if h == 0:
                    nc.scalar.copy(out=dest, in_=acc[:])
                else:
                    nc.vector.tensor_copy(out=dest, in_=acc[:])
                if place == store_banks - 1:
                    col1 = (first * COL_HALVES + b + 1) * BANK
                    nc.sync.dma_start(out=out_view[c][:, col1 - store_banks * BANK : col1], in_=result[:])

        chunks = range(BANK // K_CHUNK)

        def form_pass(g):
            units = range(g * COL_HALVES, (g + 1) * COL_HALVES)
            for parity in range(2):
                for unit in units:
                    for chunk in chunks[parity::2]:
                        start_chunk(unit, chunk)
            for unit in units:
                for chunk in chunks:
                    finish_chunk(unit, chunk)

        def transpose_round(c):
            for i in range(ROUND_PAIRS * c, ROUND_PAIRS * (c + 1)):
                transpose_pair(i)

        form_pass(0)
        transpose_round(0)
        quantise_w(0)
        quantise_w(1)
        quantise_pair(0)
        form_pass(1)
        transpose_round(1)
        quantise_w(2)
        quantise_w(3)
        transposed = AHEAD
        for i in range(PAIRS):
            if i + 1 < PAIRS:
                quantise_pair(i + 1)
            if i < PAIRS // 2:
                multiply_pair(i, ROUND_PAIRS * PAIR_BANKS)
            elif transposed < PAIRS:
                multiply_pair(i, PAIR_BANKS)
            elif i + 1 < PAIRS:
                multiply_pair(i, COL_HALVES)
            else:
                multiply_pair(i, 1)
            if transposed < PAIRS and i % REST != REST - 1:
                transpose_pair(transposed)
                transposed += 1
